import numpy as np
import ml_dtypes


def mxq(x, axis, fmt="e4m3"):
    dtype, down = {"e4m3": (ml_dtypes.float8_e4m3fn, 7), "e5m2": (ml_dtypes.float8_e5m2, 14)}[fmt]
    v = np.moveaxis(np.asarray(x, np.float32).astype(ml_dtypes.bfloat16).astype(np.float64), axis, -1)
    blocks = v.reshape(v.shape[:-1] + (-1, 32))
    amax = np.abs(blocks).max(-1, keepdims=True)
    byte = np.maximum(np.where(amax > 0, np.frexp(amax)[1] - 1 + 127, 0) - down, 1)
    scale = np.exp2(byte - 127.0)
    codes = (blocks / scale).astype(np.float32).astype(dtype).astype(np.float64)
    return np.moveaxis((codes * scale).reshape(v.shape), -1, axis)


WIDE = False


def mx_kscale(k):
    if not WIDE:
        return np.ones(k)
    levels = np.array([30, -30])
    if k % 512:
        return np.exp2(np.random.permutation(np.resize(levels, k // 32))).repeat(32)
    a = np.empty((k // 512, 16))
    for p in range(k // 512):
        a[p, :8] = np.random.permutation(np.resize(levels, 8))
        for g in range(8):
            far = levels[np.abs(levels - a[p, g]) >= 10]
            a[p, g + 8] = far[np.random.randint(len(far))]
    return np.exp2(a.ravel()).repeat(32)


BF16 = ml_dtypes.bfloat16


def bf(x):
    return np.asarray(x, np.float32).astype(BF16)


def f64(x):
    return np.asarray(x).astype(np.float64)


B, N, E, H = 1, 512, 2048, 16
D = E // H
LN_EPS = 1e-5
ROPE_BASE = 10000.0
G = D ** -0.25
WS = 0.02


def rope_cos_sin(n, d):
    inv_freq = 1.0 / (ROPE_BASE ** (f64(np.arange(0, d, 2)) / d))
    t = f64(np.arange(n))[:, None] * inv_freq[None, :]
    return np.cos(t), np.sin(t)


def apply_rope(x, cos, sin):
    x1, x2 = np.split(x, 2, axis=-1)
    c = cos[None, :, None, :]
    s = sin[None, :, None, :]
    return np.concatenate([x1 * c - x2 * s, x1 * s + x2 * c], axis=-1)


def layernorm(x, scale, bias):
    m = x.mean(-1, keepdims=True)
    v = x.var(-1, keepdims=True)
    return (x - m) / np.sqrt(v + LN_EPS) * scale + bias


def setup_inputs():
    s = mx_kscale(E)
    return {"x": bf(np.random.standard_normal((B, N, E)) * s),
            "w_qk": bf(np.random.standard_normal((E, 2 * E)) * WS / np.sqrt(E) / s[:, None]),
            "ln_scale": bf(G * (1.0 + 0.1 * np.random.standard_normal(D))),
            "ln_bias": bf(0.2 * G * np.random.standard_normal(D))}


def reference(x, w_qk, ln_scale, ln_bias):
    proj = mxq(f64(x), 2, "e5m2") @ mxq(f64(w_qk), 0, "e4m3")
    q, k = np.split(proj, 2, axis=-1)
    q = q.reshape(B, N, H, D)
    k = k.reshape(B, N, H, D)
    cos, sin = rope_cos_sin(N, D)
    q = apply_rope(q, cos, sin).transpose(0, 2, 1, 3)
    k = apply_rope(k, cos, sin).transpose(0, 2, 1, 3)
    return layernorm(q, f64(ln_scale), f64(ln_bias)), layernorm(k, f64(ln_scale), f64(ln_bias))

@@ -1,0 +1,268 @@
+import math
+from contextlib import ExitStack
+
+import concourse.mybir as mybir
+from concourse.masks import make_identity
+
+TOKENS, E, HEADS_PER_OUT, D = 512, 2048, 16, 128
+HEADS = 2 * HEADS_PER_OUT
+LN_EPS = 1e-5
+ROPE_BASE = 10000.0
+FLOPS = 2 * TOKENS * E * 2 * E
+
+F32 = mybir.dt.float32
+BF16 = mybir.dt.bfloat16
+I32 = mybir.dt.int32
+U32 = mybir.dt.uint32
+U8 = mybir.dt.uint8
+E4M3X4 = mybir.dt.float8_e4m3fn_x4
+E5M2X4 = mybir.dt.float8_e5m2_x4
+ALU = mybir.AluOpType
+ACT = mybir.ActivationFunctionType
+AXIS = mybir.AxisListType
+
+P = 128
+PACK = 4
+K_PASS = P * PACK
+PASSES = E // K_PASS
+ROWS = TOKENS // P
+HALF = D // 2
+SLAB_HEADS = 4
+SLAB = SLAB_HEADS * D
+CHUNKS = HEADS // SLAB_HEADS * PASSES
+RUN = 4
+QUANT_AHEAD = 5
+GROUP_AHEAD = 6
+LOAD_AHEAD = 12
+
+
+def tile_multiheadattention_pa_kernel(tc, x, w_qk, ln_scale, ln_bias, out_0, out_1):
+    nc = tc.nc
+    outs = (out_0, out_1)
+
+    with ExitStack() as ctx:
+        const = ctx.enter_context(tc.tile_pool(name="const", bufs=1))
+        work = ctx.enter_context(tc.tile_pool(name="work", bufs=3))
+        psum = ctx.enter_context(tc.psum_pool(name="psum", bufs=4))
+        ctx.enter_context(tc.manual_schedule())
+
+        x_rows = x[0].rearrange("(p j) k -> p j k", j=ROWS)
+        x_raw, w_raw, w_grouped, w_codes, w_scales = {}, {}, {}, {}, {}
+        proj, products, rotated, stats, centred = {}, {}, {}, {}, {}
+
+        def load_x(g):
+            x_raw[g] = const.tile([P, ROWS, K_PASS], BF16, name="x_raw%d" % g)
+            nc.sync.dma_start(out=x_raw[g][:], in_=x_rows[:, :, g * K_PASS : (g + 1) * K_PASS])
+
+        def load_w(c):
+            slab, g = divmod(c, PASSES)
+            w_raw[c] = work.tile([P, PACK, SLAB], BF16, name="w_raw", bufs=LOAD_AHEAD)
+            rows = w_qk[g * K_PASS : (g + 1) * K_PASS, slab * SLAB : (slab + 1) * SLAB]
+            nc.sync.dma_start(out=w_raw[c][:], in_=rows.rearrange("(p t) c -> p t c", t=PACK))
+
+        def group_w(c, copy):
+            w_grouped[c] = work.tile([P, SLAB, PACK], BF16, name="w_grouped", align_bytes=64)
+            copy(
+                out=w_grouped[c][:].rearrange("p (c i) t -> p c t i", i=RUN),
+                in_=w_raw[c][:].rearrange("p t (c i) -> p c t i", i=RUN),
+            )
+
+        def quantize_w(c):
+            w_codes[c] = work.tile([P, SLAB], U32, name="w_codes", bufs=10, align_bytes=64)
+            w_scales[c] = work.tile([P, SLAB], U8, name="w_scales", bufs=10, align_bytes=64)
+            nc.vector.quantize_mx(
+                out=w_codes[c][:].bitcast(E4M3X4),
+                scales=w_scales[c][:],
+                in_=w_grouped[c][:].rearrange("p c t -> p (c t)"),
+            )
+
+        load_x(0)
+        load_x(1)
+        load_w(0)
+        load_x(2)
+        load_w(1)
+        load_x(3)
+        load_w(2)
+        load_w(3)
+
+        ident = const.tile([P, P], F32)
+        make_identity(nc, ident[:])
+        one = const.tile([P, 1], F32)
+        nc.vector.memset(one[:], 1.0)
+        coarse = const.tile([P, 8], F32)
+        fine = const.tile([P, 8], F32)
+        for i in range(8):
+            nc.vector.tensor_scalar(
+                out=coarse[:, i : i + 1], in0=one[:], scalar1=ROPE_BASE ** (-i / 8) / (2 * math.pi),
+                scalar2=None, op0=ALU.mult)
+            nc.gpsimd.tensor_scalar(
+                out=fine[:, i : i + 1], in0=one[:], scalar1=ROPE_BASE ** (-i / HALF),
+                scalar2=0.0, op0=ALU.mult, op1=ALU.add)
+        position = const.tile([P, TOKENS], F32)
+        nc.gpsimd.iota(position[:], pattern=[[1, ROWS], [ROWS, P]], base=0, channel_multiplier=0,
+                       allow_small_or_imprecise_dtypes=True)
+        feature = const.tile([P, 1], F32)
+        nc.gpsimd.iota(feature[:], pattern=[[0, 1]], base=0, channel_multiplier=1,
+                       allow_small_or_imprecise_dtypes=True)
+        upper = const.tile([P, 1], F32)
+        nc.gpsimd.tensor_scalar(out=upper[:], in0=feature[:], scalar1=float(HALF), scalar2=2.0,
+                                op0=ALU.is_ge, op1=ALU.mult)
+        sin_scale = const.tile([P, 1], F32)
+        nc.gpsimd.tensor_scalar(out=sin_scale[:], in0=upper[:], scalar1=-1.0, scalar2=2 * math.pi,
+                                op0=ALU.add, op1=ALU.mult)
+        ln_rows = const.tile([P, 2, D], BF16)
+        nc.gpsimd.memset(ln_rows[:], 0.0)
+        ones = const.tile([P, P], BF16)
+        nc.gpsimd.memset(ones[:], 1.0)
+        swap = const.tile([P, 2, HALF], F32)
+        nc.gpsimd.tensor_copy(out=swap[:, 0, :], in_=ident[:, HALF:])
+        nc.gpsimd.tensor_copy(out=swap[:, 1, :], in_=ident[:, :HALF])
+        nc.sync.dma_start(out=ln_rows[0:1, 0, :], in_=ln_scale.unsqueeze(0))
+        nc.sync.dma_start(out=ln_rows[0:1, 1, :], in_=ln_bias.unsqueeze(0))
+        for c in range(PASSES, LOAD_AHEAD):
+            load_w(c)
+
+        rates = const.tile([P, 8, 8], F32)
+        nc.vector.tensor_tensor(
+            out=rates[:], in0=coarse[:].unsqueeze(2).to_broadcast([P, 8, 8]),
+            in1=fine[:].unsqueeze(1).to_broadcast([P, 8, 8]), op=ALU.mult)
+        picked = const.tile([P, 2, HALF], F32)
+        nc.vector.tensor_tensor(
+            out=picked[:], in0=ident[:].rearrange("p (a j) -> p a j", a=2),
+            in1=rates[:].rearrange("p a b -> p (a b)").unsqueeze(1).to_broadcast([P, 2, HALF]), op=ALU.mult)
+        rate = const.tile([P, 1], F32)
+        nc.vector.tensor_reduce(out=rate[:], in_=picked[:].rearrange("p a j -> p (a j)"), axis=AXIS.X, op=ALU.add)
+        turns = const.tile([P, 2, TOKENS], F32)
+        nc.vector.tensor_scalar(out=turns[:, 0, :], in0=position[:], scalar1=rate[:], scalar2=0.25,
+                                op0=ALU.mult, op1=ALU.add)
+        nc.vector.tensor_scalar(out=turns[:, 1, :], in0=position[:], scalar1=rate[:], scalar2=None,
+                                op0=ALU.mult)
+        whole = const.tile([P, 2, TOKENS], I32)
+        nc.vector.tensor_copy(out=whole[:], in_=turns[:])
+        fraction = const.tile([P, 2, TOKENS], F32)
+        nc.vector.tensor_tensor(out=fraction[:], in0=turns[:], in1=whole[:], op=ALU.subtract)
+        negated = const.tile([P, 2, TOKENS], F32)
+        nc.vector.scalar_tensor_tensor(out=negated[:], in0=fraction[:], scalar=0.5, in1=fraction[:],
+                                       op0=ALU.is_gt, op1=ALU.subtract)
+        table = const.tile([P, 2, TOKENS], F32)
+
+        x_codes = const.tile([P, PASSES, TOKENS], U32, align_bytes=64)
+        x_scales = const.tile([P, PASSES, TOKENS], U8, align_bytes=64)
+        x_grouped = {}
+
+        def transpose_x(g):
+            words = x_raw[g][:].rearrange("p j k -> p (j k)").bitcast(F32)
+            x_grouped[g] = const.tile([P, TOKENS * PACK], BF16, name="x_grouped%d" % g, align_bytes=64)
+            pairs = x_grouped[g][:].bitcast(F32).rearrange("p (j r u) -> p j r u", j=ROWS, u=2)
+            for a in range(ROWS // 2):
+                bank = psum.tile([P, 2, 2, P], F32, name="bank_a")
+                for jj in range(2):
+                    first = (2 * a + jj) * (K_PASS // 2)
+                    for u in range(2):
+                        nc.tensor.transpose(bank[:, jj, u, :], words[:, first + u : first + K_PASS // 2 : 2], ident[:])
+                nc.scalar.copy(out=pairs[:, 2 * a : 2 * a + 2], in_=bank[:].rearrange("p j u r -> p j r u"))
+
+        def quantize_x(g):
+            nc.vector.quantize_mx(out=x_codes[:, g, :].bitcast(E5M2X4), scales=x_scales[:, g, :], in_=x_grouped[g][:])
+
+        def multiply(h):
+            slab, hh = divmod(h, SLAB_HEADS)
+            cols = slice(hh * D, (hh + 1) * D)
+            proj[h] = psum.tile([P, TOKENS], F32, name="bank_b")
+            for g in range(PASSES):
+                c = slab * PASSES + g
+                nc.tensor.matmul_mx(
+                    out=proj[h][:], lhsT=w_codes[c][:, cols].bitcast(E4M3X4), lhsT_scale=w_scales[c][:, cols],
+                    rhs=x_codes[:, g, :].bitcast(E5M2X4), rhs_scale=x_scales[:, g, :],
+                    start=(g == 0), stop=(g == PASSES - 1))
+
+        def rope_product(h, which):
+            products[h, which] = work.tile([P, TOKENS], F32, name="product%d" % which)
+            nc.vector.tensor_tensor(out=products[h, which][:], in0=proj[h][:], in1=table[:, which, :], op=ALU.mult)
+
+        def rope_sum(h):
+            rotated[h] = psum.tile([P, ROWS, D], F32, name="bank_a")
+            for j in range(ROWS):
+                cols = slice(j * P, (j + 1) * P)
+                nc.tensor.matmul(rotated[h][:, j, :], lhsT=products[h, 0][:, cols], rhs=ident[:],
+                                 start=True, stop=False, is_transpose=True)
+                nc.tensor.matmul(rotated[h][:, j, :], lhsT=products[h, 1][:, cols],
+                                 rhs=swap[:].rearrange("p a j -> p (a j)"),
+                                 start=False, stop=True, is_transpose=True)
+
+        def statistics(h):
+            stats[h] = work.tile([P, ROWS, 3], F32, name="stats")
+            for a in range(ROWS // 2):
+                nc.vector.bn_stats(
+                    out=stats[h][:, 2 * a : 2 * a + 2, :].rearrange("p j s -> p (j s)"),
+                    in_=rotated[h][:, 2 * a : 2 * a + 2, :].rearrange("p j d -> p d j"))
+
+        def centre(h):
+            centred[h] = work.tile([P, ROWS, D], F32, name="centred")
+            for j in range(ROWS):
+                nc.vector.scalar_tensor_tensor(
+                    out=centred[h][:, j, :], in0=rotated[h][:, j, :], scalar=stats[h][:, j, 1:2], in1=gain[:],
+                    op0=ALU.subtract, op1=ALU.mult)
+
+        def finish(h):
+            rstd = work.tile([P, ROWS], F32, name="rstd")
+            nc.scalar.activation(out=rstd[:], in_=stats[h][:, :, 2], func=ACT.Abs_reciprocal_sqrt,
+                                 scale=1.0 / D, bias=LN_EPS)
+            scaled = work.tile([P, ROWS, D], F32, name="scaled")
+            for j in range(ROWS):
+                nc.scalar.activation(out=scaled[:, j, :], in_=centred[h][:, j, :], func=ACT.Copy,
+                                     scale=rstd[:, j : j + 1])
+            result = work.tile([P, ROWS, D], F32, name="result", bufs=4)
+            nc.gpsimd.tensor_tensor(out=result[:], in0=scaled[:], in1=bias[:], op=ALU.add)
+            which, head = divmod(h, HEADS_PER_OUT)
+            nc.sync.dma_start(out=outs[which][0, head].rearrange("(p j) d -> p j d", j=ROWS), in_=result[:])
+
+        transpose_x(0)
+        transpose_x(1)
+        nc.scalar.activation(out=table[:, 0, :], in_=negated[:, 0, :], func=ACT.Sin, scale=-2 * math.pi)
+        nc.scalar.activation(out=table[:, 1, :], in_=negated[:, 1, :], func=ACT.Sin, scale=sin_scale[:])
+        group_w(0, nc.vector.tensor_copy)
+        quantize_x(0)
+        transpose_x(2)
+        quantize_w(0)
+        group_w(1, nc.vector.tensor_copy)
+        quantize_x(1)
+        transpose_x(3)
+        quantize_w(1)
+        group_w(2, nc.vector.tensor_copy)
+        quantize_x(2)
+        group_w(3, nc.scalar.copy)
+        quantize_w(2)
+        quantize_x(3)
+        spread = psum.tile([P, 2, D], F32, name="bank_a")
+        nc.tensor.matmul(spread[:].rearrange("p a d -> p (a d)"), lhsT=ones[:],
+                         rhs=ln_rows[:].rearrange("p a d -> p (a d)"), start=True, stop=True)
+        group_w(4, nc.vector.tensor_copy)
+        quantize_w(3)
+        multiply(0)
+        gain = const.tile([P, D], F32)
+        bias = const.tile([P, ROWS, D], F32)
+        nc.scalar.copy(out=gain[:], in_=spread[:, 0, :])
+        nc.scalar.copy(out=bias[:], in_=spread[:, 1:2, :].to_broadcast([P, ROWS, D]))
+        group_w(5, nc.scalar.copy)
+        quantize_w(4)
+
+        for s in range(HEADS + 1):
+            if s + LOAD_AHEAD < CHUNKS:
+                load_w(s + LOAD_AHEAD)
+            if s + 1 < HEADS:
+                multiply(s + 1)
+            if s + GROUP_AHEAD < CHUNKS:
+                group_w(s + GROUP_AHEAD, nc.scalar.copy)
+            if s < HEADS:
+                rope_product(s, 0)
+            if s > 0:
+                statistics(s - 1)
+            if s < HEADS:
+                rope_product(s, 1)
+                rope_sum(s)
+            if s > 0:
+                centre(s - 1)
+                finish(s - 1)
+            if s + QUANT_AHEAD < CHUNKS:
+                quantize_w(s + QUANT_AHEAD)

@@ -27,13 +27,16 @@ K_PASS = P * PACK
 PASSES = E // K_PASS
 ROWS = TOKENS // P
 HALF = D // 2
-SLAB_HEADS = 4
-SLAB = SLAB_HEADS * D
-CHUNKS = HEADS // SLAB_HEADS * PASSES
+SLAB_HEADS = (2, 2) + (4,) * 7
+SLAB_FIRST = [sum(SLAB_HEADS[:i]) for i in range(len(SLAB_HEADS))]
+SLAB_OF = [i for i, n in enumerate(SLAB_HEADS) for head in range(n)]
+CHUNKS = len(SLAB_HEADS) * PASSES
 RUN = 4
-QUANT_AHEAD = 5
-GROUP_AHEAD = 6
+QUANT_AHEAD = 2
+GROUP_AHEAD = 3
 LOAD_AHEAD = 12
+POOL_COLS = 64
+NORM_LAG = 2
 
 
 def tile_multiheadattention_pa_kernel(tc, x, w_qk, ln_scale, ln_bias, out_0, out_1):
@@ -56,24 +59,45 @@ def tile_multiheadattention_pa_kernel(tc, x, w_qk, ln_scale, ln_bias, out_0, out
 
         def load_w(c):
             slab, g = divmod(c, PASSES)
-            w_raw[c] = work.tile([P, PACK, SLAB], BF16, name="w_raw", bufs=LOAD_AHEAD)
-            rows = w_qk[g * K_PASS : (g + 1) * K_PASS, slab * SLAB : (slab + 1) * SLAB]
+            first, width = SLAB_FIRST[slab] * D, SLAB_HEADS[slab] * D
+            w_raw[c] = work.tile([P, PACK, width], BF16, name="w_raw", bufs=LOAD_AHEAD)
+            rows = w_qk[g * K_PASS : (g + 1) * K_PASS, first : first + width]
             nc.sync.dma_start(out=w_raw[c][:], in_=rows.rearrange("(p t) c -> p t c", t=PACK))
 
-        def group_w(c, copy):
-            w_grouped[c] = work.tile([P, SLAB, PACK], BF16, name="w_grouped", align_bytes=64)
+        def raw_cols(h, g, first, last):
+            slab = SLAB_OF[h]
+            offset = (h - SLAB_FIRST[slab]) * D
+            return w_raw[slab * PASSES + g][:, :, offset + first : offset + last]
+
+        def new_group(h):
+            w_grouped[h] = work.tile([P, PASSES, D, PACK], BF16, name="w_grouped", bufs=4, align_bytes=64)
+
+        def group_w(h, g, copy, first=0):
             copy(
-                out=w_grouped[c][:].rearrange("p (c i) t -> p c t i", i=RUN),
-                in_=w_raw[c][:].rearrange("p t (c i) -> p c t i", i=RUN),
+                out=w_grouped[h][:, g, first:, :].rearrange("p (c i) t -> p c t i", i=RUN),
+                in_=raw_cols(h, g, first, D).rearrange("p t (c i) -> p c t i", i=RUN),
             )
 
-        def quantize_w(c):
-            w_codes[c] = work.tile([P, SLAB], U32, name="w_codes", bufs=10, align_bytes=64)
-            w_scales[c] = work.tile([P, SLAB], U8, name="w_scales", bufs=10, align_bytes=64)
+        def group_w_pool(h):
+            new_group(h)
+            nc.gpsimd.tensor_copy(out=w_grouped[h][:, 0, :POOL_COLS, :],
+                                  in_=raw_cols(h, 0, 0, POOL_COLS).rearrange("p t c -> p c t"))
+
+        def group_w_scalar(h):
+            for g in range(PASSES):
+                group_w(h, g, nc.scalar.copy, POOL_COLS if g == 0 else 0)
+
+        def new_codes(h):
+            w_codes[h] = work.tile([P, PASSES, D], U32, name="w_codes", bufs=4, align_bytes=64)
+            w_scales[h] = work.tile([P, PASSES, D], U8, name="w_scales", bufs=4, align_bytes=64)
+
+        def quantize_w(h, first=0, last=PASSES):
+            if first == 0:
+                new_codes(h)
             nc.vector.quantize_mx(
-                out=w_codes[c][:].bitcast(E4M3X4),
-                scales=w_scales[c][:],
-                in_=w_grouped[c][:].rearrange("p c t -> p (c t)"),
+                out=w_codes[h][:, first:last, :].rearrange("p g c -> p (g c)").bitcast(E4M3X4),
+                scales=w_scales[h][:, first:last, :].rearrange("p g c -> p (g c)"),
+                in_=w_grouped[h][:, first:last].rearrange("p g c t -> p (g c t)"),
             )
 
         load_x(0)
@@ -150,7 +174,7 @@ def tile_multiheadattention_pa_kernel(tc, x, w_qk, ln_scale, ln_bias, out_0, out
         x_scales = const.tile([P, PASSES, TOKENS], U8, align_bytes=64)
         x_grouped = {}
 
-        def transpose_x(g):
+        def transpose_x(g, last_copy):
             words = x_raw[g][:].rearrange("p j k -> p (j k)").bitcast(F32)
             x_grouped[g] = const.tile([P, TOKENS * PACK], BF16, name="x_grouped%d" % g, align_bytes=64)
             pairs = x_grouped[g][:].bitcast(F32).rearrange("p (j r u) -> p j r u", j=ROWS, u=2)
@@ -160,21 +184,19 @@ def tile_multiheadattention_pa_kernel(tc, x, w_qk, ln_scale, ln_bias, out_0, out
                     first = (2 * a + jj) * (K_PASS // 2)
                     for u in range(2):
                         nc.tensor.transpose(bank[:, jj, u, :], words[:, first + u : first + K_PASS // 2 : 2], ident[:])
-                nc.scalar.copy(out=pairs[:, 2 * a : 2 * a + 2], in_=bank[:].rearrange("p j u r -> p j r u"))
+                copy = nc.scalar.copy if a == 0 else last_copy
+                copy(out=pairs[:, 2 * a : 2 * a + 2], in_=bank[:].rearrange("p j u r -> p j r u"))
 
         def quantize_x(g):
             nc.vector.quantize_mx(out=x_codes[:, g, :].bitcast(E5M2X4), scales=x_scales[:, g, :], in_=x_grouped[g][:])
 
-        def multiply(h):
-            slab, hh = divmod(h, SLAB_HEADS)
-            cols = slice(hh * D, (hh + 1) * D)
-            proj[h] = psum.tile([P, TOKENS], F32, name="bank_b")
-            for g in range(PASSES):
-                c = slab * PASSES + g
-                nc.tensor.matmul_mx(
-                    out=proj[h][:], lhsT=w_codes[c][:, cols].bitcast(E4M3X4), lhsT_scale=w_scales[c][:, cols],
-                    rhs=x_codes[:, g, :].bitcast(E5M2X4), rhs_scale=x_scales[:, g, :],
-                    start=(g == 0), stop=(g == PASSES - 1))
+        def multiply_pass(h, g):
+            if g == 0:
+                proj[h] = psum.tile([P, TOKENS], F32, name="bank_b")
+            nc.tensor.matmul_mx(
+                out=proj[h][:], lhsT=w_codes[h][:, g, :].bitcast(E4M3X4), lhsT_scale=w_scales[h][:, g, :],
+                rhs=x_codes[:, g, :].bitcast(E5M2X4), rhs_scale=x_scales[:, g, :],
+                start=(g == 0), stop=(g == PASSES - 1))
 
         def rope_product(h, which):
             products[h, which] = work.tile([P, TOKENS], F32, name="product%d" % which)
@@ -217,52 +239,55 @@ def tile_multiheadattention_pa_kernel(tc, x, w_qk, ln_scale, ln_bias, out_0, out
             which, head = divmod(h, HEADS_PER_OUT)
             nc.sync.dma_start(out=outs[which][0, head].rearrange("(p j) d -> p j d", j=ROWS), in_=result[:])
 
-        transpose_x(0)
-        transpose_x(1)
+        new_group(0)
+        new_group(1)
+        transpose_x(0, nc.scalar.copy)
+        transpose_x(1, nc.scalar.copy)
         nc.scalar.activation(out=table[:, 0, :], in_=negated[:, 0, :], func=ACT.Sin, scale=-2 * math.pi)
+        transpose_x(2, nc.scalar.copy)
         nc.scalar.activation(out=table[:, 1, :], in_=negated[:, 1, :], func=ACT.Sin, scale=sin_scale[:])
-        group_w(0, nc.vector.tensor_copy)
-        quantize_x(0)
-        transpose_x(2)
-        quantize_w(0)
-        group_w(1, nc.vector.tensor_copy)
-        quantize_x(1)
-        transpose_x(3)
-        quantize_w(1)
-        group_w(2, nc.vector.tensor_copy)
-        quantize_x(2)
-        group_w(3, nc.scalar.copy)
-        quantize_w(2)
-        quantize_x(3)
+        for g in range(PASSES):
+            group_w(0, g, nc.vector.tensor_copy)
+            group_w(1, g, nc.vector.tensor_copy)
+            if g == PASSES - 1:
+                transpose_x(g, nc.vector.tensor_copy)
+            quantize_w(0, g, g + 1)
+            quantize_x(g)
+            quantize_w(1, g, g + 1)
+        for h in range(2):
+            for g in range(PASSES):
+                multiply_pass(h, g)
         spread = psum.tile([P, 2, D], F32, name="bank_a")
         nc.tensor.matmul(spread[:].rearrange("p a d -> p (a d)"), lhsT=ones[:],
                          rhs=ln_rows[:].rearrange("p a d -> p (a d)"), start=True, stop=True)
-        group_w(4, nc.vector.tensor_copy)
-        quantize_w(3)
-        multiply(0)
+        group_w_pool(2)
+        group_w_scalar(2)
         gain = const.tile([P, D], F32)
         bias = const.tile([P, ROWS, D], F32)
         nc.scalar.copy(out=gain[:], in_=spread[:, 0, :])
         nc.scalar.copy(out=bias[:], in_=spread[:, 1:2, :].to_broadcast([P, ROWS, D]))
-        group_w(5, nc.scalar.copy)
-        quantize_w(4)
+        group_w_pool(3)
 
-        for s in range(HEADS + 1):
+        for s in range(HEADS + NORM_LAG):
+            n = s - NORM_LAG
             if s + LOAD_AHEAD < CHUNKS:
                 load_w(s + LOAD_AHEAD)
-            if s + 1 < HEADS:
-                multiply(s + 1)
-            if s + GROUP_AHEAD < CHUNKS:
-                group_w(s + GROUP_AHEAD, nc.scalar.copy)
+            if 2 <= s + 1 < HEADS:
+                for g in range(PASSES):
+                    multiply_pass(s + 1, g)
+            if s + GROUP_AHEAD < HEADS:
+                group_w_scalar(s + GROUP_AHEAD)
             if s < HEADS:
                 rope_product(s, 0)
-            if s > 0:
-                statistics(s - 1)
+            if n >= 0:
+                statistics(n)
             if s < HEADS:
                 rope_product(s, 1)
                 rope_sum(s)
-            if s > 0:
-                centre(s - 1)
-                finish(s - 1)
-            if s + QUANT_AHEAD < CHUNKS:
+            if n >= 0:
+                centre(n)
+                finish(n)
+            if s + GROUP_AHEAD + 1 < HEADS:
+                group_w_pool(s + GROUP_AHEAD + 1)
+            if s + QUANT_AHEAD < HEADS:
                 quantize_w(s + QUANT_AHEAD)

import math
from contextlib import ExitStack

import concourse.mybir as mybir
from concourse.masks import make_identity

TOKENS, E, HEADS_PER_OUT, D = 512, 2048, 16, 128
HEADS = 2 * HEADS_PER_OUT
LN_EPS = 1e-5
ROPE_BASE = 10000.0
FLOPS = 2 * TOKENS * E * 2 * E

F32 = mybir.dt.float32
BF16 = mybir.dt.bfloat16
I32 = mybir.dt.int32
U32 = mybir.dt.uint32
U8 = mybir.dt.uint8
E4M3X4 = mybir.dt.float8_e4m3fn_x4
E5M2X4 = mybir.dt.float8_e5m2_x4
ALU = mybir.AluOpType
ACT = mybir.ActivationFunctionType
AXIS = mybir.AxisListType

P = 128
PACK = 4
K_PASS = P * PACK
PASSES = E // K_PASS
ROWS = TOKENS // P
HALF = D // 2
SLAB_HEADS = (2, 2) + (4,) * 7
SLAB_FIRST = [sum(SLAB_HEADS[:i]) for i in range(len(SLAB_HEADS))]
SLAB_OF = [i for i, n in enumerate(SLAB_HEADS) for head in range(n)]
CHUNKS = len(SLAB_HEADS) * PASSES
RUN = 4
QUANT_AHEAD = 2
GROUP_AHEAD = 3
LOAD_AHEAD = 12
POOL_COLS = 64
NORM_LAG = 2


def tile_multiheadattention_pa_kernel(tc, x, w_qk, ln_scale, ln_bias, out_0, out_1):
    nc = tc.nc
    outs = (out_0, out_1)

    with ExitStack() as ctx:
        const = ctx.enter_context(tc.tile_pool(name="const", bufs=1))
        work = ctx.enter_context(tc.tile_pool(name="work", bufs=3))
        psum = ctx.enter_context(tc.psum_pool(name="psum", bufs=4))
        ctx.enter_context(tc.manual_schedule())

        x_rows = x[0].rearrange("(p j) k -> p j k", j=ROWS)
        x_raw, w_raw, w_grouped, w_codes, w_scales = {}, {}, {}, {}, {}
        proj, products, rotated, stats, centred = {}, {}, {}, {}, {}

        def load_x(g):
            x_raw[g] = const.tile([P, ROWS, K_PASS], BF16, name="x_raw%d" % g)
            nc.sync.dma_start(out=x_raw[g][:], in_=x_rows[:, :, g * K_PASS : (g + 1) * K_PASS])

        def load_w(c):
            slab, g = divmod(c, PASSES)
            first, width = SLAB_FIRST[slab] * D, SLAB_HEADS[slab] * D
            w_raw[c] = work.tile([P, PACK, width], BF16, name="w_raw", bufs=LOAD_AHEAD)
            rows = w_qk[g * K_PASS : (g + 1) * K_PASS, first : first + width]
            nc.sync.dma_start(out=w_raw[c][:], in_=rows.rearrange("(p t) c -> p t c", t=PACK))

        def raw_cols(h, g, first, last):
            slab = SLAB_OF[h]
            offset = (h - SLAB_FIRST[slab]) * D
            return w_raw[slab * PASSES + g][:, :, offset + first : offset + last]

        def new_group(h):
            w_grouped[h] = work.tile([P, PASSES, D, PACK], BF16, name="w_grouped", bufs=4, align_bytes=64)

        def group_w(h, g, copy, first=0):
            copy(
                out=w_grouped[h][:, g, first:, :].rearrange("p (c i) t -> p c t i", i=RUN),
                in_=raw_cols(h, g, first, D).rearrange("p t (c i) -> p c t i", i=RUN),
            )

        def group_w_pool(h):
            new_group(h)
            nc.gpsimd.tensor_copy(out=w_grouped[h][:, 0, :POOL_COLS, :],
                                  in_=raw_cols(h, 0, 0, POOL_COLS).rearrange("p t c -> p c t"))

        def group_w_scalar(h):
            for g in range(PASSES):
                group_w(h, g, nc.scalar.copy, POOL_COLS if g == 0 else 0)

        def new_codes(h):
            w_codes[h] = work.tile([P, PASSES, D], U32, name="w_codes", bufs=4, align_bytes=64)
            w_scales[h] = work.tile([P, PASSES, D], U8, name="w_scales", bufs=4, align_bytes=64)

        def quantize_w(h, first=0, last=PASSES):
            if first == 0:
                new_codes(h)
            nc.vector.quantize_mx(
                out=w_codes[h][:, first:last, :].rearrange("p g c -> p (g c)").bitcast(E4M3X4),
                scales=w_scales[h][:, first:last, :].rearrange("p g c -> p (g c)"),
                in_=w_grouped[h][:, first:last].rearrange("p g c t -> p (g c t)"),
            )

        load_x(0)
        load_x(1)
        load_w(0)
        load_x(2)
        load_w(1)
        load_x(3)
        load_w(2)
        load_w(3)

        ident = const.tile([P, P], F32)
        make_identity(nc, ident[:])
        one = const.tile([P, 1], F32)
        nc.vector.memset(one[:], 1.0)
        coarse = const.tile([P, 8], F32)
        fine = const.tile([P, 8], F32)
        for i in range(8):
            nc.vector.tensor_scalar(
                out=coarse[:, i : i + 1], in0=one[:], scalar1=ROPE_BASE ** (-i / 8) / (2 * math.pi),
                scalar2=None, op0=ALU.mult)
            nc.gpsimd.tensor_scalar(
                out=fine[:, i : i + 1], in0=one[:], scalar1=ROPE_BASE ** (-i / HALF),
                scalar2=0.0, op0=ALU.mult, op1=ALU.add)
        position = const.tile([P, TOKENS], F32)
        nc.gpsimd.iota(position[:], pattern=[[1, ROWS], [ROWS, P]], base=0, channel_multiplier=0,
                       allow_small_or_imprecise_dtypes=True)
        feature = const.tile([P, 1], F32)
        nc.gpsimd.iota(feature[:], pattern=[[0, 1]], base=0, channel_multiplier=1,
                       allow_small_or_imprecise_dtypes=True)
        upper = const.tile([P, 1], F32)
        nc.gpsimd.tensor_scalar(out=upper[:], in0=feature[:], scalar1=float(HALF), scalar2=2.0,
                                op0=ALU.is_ge, op1=ALU.mult)
        sin_scale = const.tile([P, 1], F32)
        nc.gpsimd.tensor_scalar(out=sin_scale[:], in0=upper[:], scalar1=-1.0, scalar2=2 * math.pi,
                                op0=ALU.add, op1=ALU.mult)
        ln_rows = const.tile([P, 2, D], BF16)
        nc.gpsimd.memset(ln_rows[:], 0.0)
        ones = const.tile([P, P], BF16)
        nc.gpsimd.memset(ones[:], 1.0)
        swap = const.tile([P, 2, HALF], F32)
        nc.gpsimd.tensor_copy(out=swap[:, 0, :], in_=ident[:, HALF:])
        nc.gpsimd.tensor_copy(out=swap[:, 1, :], in_=ident[:, :HALF])
        nc.sync.dma_start(out=ln_rows[0:1, 0, :], in_=ln_scale.unsqueeze(0))
        nc.sync.dma_start(out=ln_rows[0:1, 1, :], in_=ln_bias.unsqueeze(0))
        for c in range(PASSES, LOAD_AHEAD):
            load_w(c)

        rates = const.tile([P, 8, 8], F32)
        nc.vector.tensor_tensor(
            out=rates[:], in0=coarse[:].unsqueeze(2).to_broadcast([P, 8, 8]),
            in1=fine[:].unsqueeze(1).to_broadcast([P, 8, 8]), op=ALU.mult)
        picked = const.tile([P, 2, HALF], F32)
        nc.vector.tensor_tensor(
            out=picked[:], in0=ident[:].rearrange("p (a j) -> p a j", a=2),
            in1=rates[:].rearrange("p a b -> p (a b)").unsqueeze(1).to_broadcast([P, 2, HALF]), op=ALU.mult)
        rate = const.tile([P, 1], F32)
        nc.vector.tensor_reduce(out=rate[:], in_=picked[:].rearrange("p a j -> p (a j)"), axis=AXIS.X, op=ALU.add)
        turns = const.tile([P, 2, TOKENS], F32)
        nc.vector.tensor_scalar(out=turns[:, 0, :], in0=position[:], scalar1=rate[:], scalar2=0.25,
                                op0=ALU.mult, op1=ALU.add)
        nc.vector.tensor_scalar(out=turns[:, 1, :], in0=position[:], scalar1=rate[:], scalar2=None,
                                op0=ALU.mult)
        whole = const.tile([P, 2, TOKENS], I32)
        nc.vector.tensor_copy(out=whole[:], in_=turns[:])
        fraction = const.tile([P, 2, TOKENS], F32)
        nc.vector.tensor_tensor(out=fraction[:], in0=turns[:], in1=whole[:], op=ALU.subtract)
        negated = const.tile([P, 2, TOKENS], F32)
        nc.vector.scalar_tensor_tensor(out=negated[:], in0=fraction[:], scalar=0.5, in1=fraction[:],
                                       op0=ALU.is_gt, op1=ALU.subtract)
        table = const.tile([P, 2, TOKENS], F32)

        x_codes = const.tile([P, PASSES, TOKENS], U32, align_bytes=64)
        x_scales = const.tile([P, PASSES, TOKENS], U8, align_bytes=64)
        x_grouped = {}

        def transpose_x(g, last_copy):
            words = x_raw[g][:].rearrange("p j k -> p (j k)").bitcast(F32)
            x_grouped[g] = const.tile([P, TOKENS * PACK], BF16, name="x_grouped%d" % g, align_bytes=64)
            pairs = x_grouped[g][:].bitcast(F32).rearrange("p (j r u) -> p j r u", j=ROWS, u=2)
            for a in range(ROWS // 2):
                bank = psum.tile([P, 2, 2, P], F32, name="bank_a")
                for jj in range(2):
                    first = (2 * a + jj) * (K_PASS // 2)
                    for u in range(2):
                        nc.tensor.transpose(bank[:, jj, u, :], words[:, first + u : first + K_PASS // 2 : 2], ident[:])
                copy = nc.scalar.copy if a == 0 else last_copy
                copy(out=pairs[:, 2 * a : 2 * a + 2], in_=bank[:].rearrange("p j u r -> p j r u"))

        def quantize_x(g):
            nc.vector.quantize_mx(out=x_codes[:, g, :].bitcast(E5M2X4), scales=x_scales[:, g, :], in_=x_grouped[g][:])

        def multiply_pass(h, g):
            if g == 0:
                proj[h] = psum.tile([P, TOKENS], F32, name="bank_b")
            nc.tensor.matmul_mx(
                out=proj[h][:], lhsT=w_codes[h][:, g, :].bitcast(E4M3X4), lhsT_scale=w_scales[h][:, g, :],
                rhs=x_codes[:, g, :].bitcast(E5M2X4), rhs_scale=x_scales[:, g, :],
                start=(g == 0), stop=(g == PASSES - 1))

        def rope_product(h, which):
            products[h, which] = work.tile([P, TOKENS], F32, name="product%d" % which)
            nc.vector.tensor_tensor(out=products[h, which][:], in0=proj[h][:], in1=table[:, which, :], op=ALU.mult)

        def rope_sum(h):
            rotated[h] = psum.tile([P, ROWS, D], F32, name="bank_a")
            for j in range(ROWS):
                cols = slice(j * P, (j + 1) * P)
                nc.tensor.matmul(rotated[h][:, j, :], lhsT=products[h, 0][:, cols], rhs=ident[:],
                                 start=True, stop=False, is_transpose=True)
                nc.tensor.matmul(rotated[h][:, j, :], lhsT=products[h, 1][:, cols],
                                 rhs=swap[:].rearrange("p a j -> p (a j)"),
                                 start=False, stop=True, is_transpose=True)

        def statistics(h):
            stats[h] = work.tile([P, ROWS, 3], F32, name="stats")
            for a in range(ROWS // 2):
                nc.vector.bn_stats(
                    out=stats[h][:, 2 * a : 2 * a + 2, :].rearrange("p j s -> p (j s)"),
                    in_=rotated[h][:, 2 * a : 2 * a + 2, :].rearrange("p j d -> p d j"))

        def centre(h):
            centred[h] = work.tile([P, ROWS, D], F32, name="centred")
            for j in range(ROWS):
                nc.vector.scalar_tensor_tensor(
                    out=centred[h][:, j, :], in0=rotated[h][:, j, :], scalar=stats[h][:, j, 1:2], in1=gain[:],
                    op0=ALU.subtract, op1=ALU.mult)

        def finish(h):
            rstd = work.tile([P, ROWS], F32, name="rstd")
            nc.scalar.activation(out=rstd[:], in_=stats[h][:, :, 2], func=ACT.Abs_reciprocal_sqrt,
                                 scale=1.0 / D, bias=LN_EPS)
            scaled = work.tile([P, ROWS, D], F32, name="scaled")
            for j in range(ROWS):
                nc.scalar.activation(out=scaled[:, j, :], in_=centred[h][:, j, :], func=ACT.Copy,
                                     scale=rstd[:, j : j + 1])
            result = work.tile([P, ROWS, D], F32, name="result", bufs=4)
            nc.gpsimd.tensor_tensor(out=result[:], in0=scaled[:], in1=bias[:], op=ALU.add)
            which, head = divmod(h, HEADS_PER_OUT)
            nc.sync.dma_start(out=outs[which][0, head].rearrange("(p j) d -> p j d", j=ROWS), in_=result[:])

        new_group(0)
        new_group(1)
        transpose_x(0, nc.scalar.copy)
        transpose_x(1, nc.scalar.copy)
        nc.scalar.activation(out=table[:, 0, :], in_=negated[:, 0, :], func=ACT.Sin, scale=-2 * math.pi)
        transpose_x(2, nc.scalar.copy)
        nc.scalar.activation(out=table[:, 1, :], in_=negated[:, 1, :], func=ACT.Sin, scale=sin_scale[:])
        for g in range(PASSES):
            group_w(0, g, nc.vector.tensor_copy)
            group_w(1, g, nc.vector.tensor_copy)
            if g == PASSES - 1:
                transpose_x(g, nc.vector.tensor_copy)
            quantize_w(0, g, g + 1)
            quantize_x(g)
            quantize_w(1, g, g + 1)
        for h in range(2):
            for g in range(PASSES):
                multiply_pass(h, g)
        spread = psum.tile([P, 2, D], F32, name="bank_a")
        nc.tensor.matmul(spread[:].rearrange("p a d -> p (a d)"), lhsT=ones[:],
                         rhs=ln_rows[:].rearrange("p a d -> p (a d)"), start=True, stop=True)
        group_w_pool(2)
        group_w_scalar(2)
        gain = const.tile([P, D], F32)
        bias = const.tile([P, ROWS, D], F32)
        nc.scalar.copy(out=gain[:], in_=spread[:, 0, :])
        nc.scalar.copy(out=bias[:], in_=spread[:, 1:2, :].to_broadcast([P, ROWS, D]))
        group_w_pool(3)

        for s in range(HEADS + NORM_LAG):
            n = s - NORM_LAG
            if s + LOAD_AHEAD < CHUNKS:
                load_w(s + LOAD_AHEAD)
            if 2 <= s + 1 < HEADS:
                for g in range(PASSES):
                    multiply_pass(s + 1, g)
            if s + GROUP_AHEAD < HEADS:
                group_w_scalar(s + GROUP_AHEAD)
            if s < HEADS:
                rope_product(s, 0)
            if n >= 0:
                statistics(n)
            if s < HEADS:
                rope_product(s, 1)
                rope_sum(s)
            if n >= 0:
                centre(n)
                finish(n)
            if s + GROUP_AHEAD + 1 < HEADS:
                group_w_pool(s + GROUP_AHEAD + 1)
            if s + QUANT_AHEAD < HEADS:
                quantize_w(s + QUANT_AHEAD)
